import numpy as np
import ml_dtypes


BF16 = ml_dtypes.bfloat16


def bf(x):
    return np.asarray(x, np.float32).astype(BF16)


def f64(x):
    return np.asarray(x).astype(np.float64)


E2M1 = np.array([0.0, 0.5, 1.0, 1.5, 2.0, 3.0, 4.0, 6.0, -0.0, -0.5, -1.0, -1.5, -2.0, -3.0, -4.0, -6.0])


def pack_weight(w, fmt):
    k, n = w.shape
    w = f64(bf(w)).reshape(k // 32, 32, n)
    amax = np.abs(w).max(1)
    if fmt == "e4m3":
        byte = np.frexp(amax)[1] - 1 + 127 - 7
    else:
        mant, ex = np.frexp(amax / 6.0)
        byte = np.where(mant > 0.5, ex, ex - 1) + 127
    byte = np.clip(np.where(amax > 0, byte, 1), 1, 254)
    scaled = (w * np.exp2(127.0 - byte)[:, None, :]).reshape(k, n).astype(np.float32)
    by_word = np.ascontiguousarray(scaled.reshape(k // 512, 128, 4, n).transpose(0, 1, 3, 2))
    if fmt == "e4m3":
        words = by_word.astype(ml_dtypes.float8_e4m3fn).view(np.uint8)
    else:
        c = by_word.astype(ml_dtypes.float4_e2m1fn).view(np.uint8) & 0xF
        words = c[..., 0::2] | (c[..., 1::2] << 4)
    return np.ascontiguousarray(words), np.ascontiguousarray(byte.astype(np.uint8).reshape(k // 512, 16, n))


def unpack_weight(words, scales, fmt):
    g, p, n, _ = words.shape
    if fmt == "e4m3":
        vals = np.ascontiguousarray(words).view(ml_dtypes.float8_e4m3fn).astype(np.float64)
    else:
        nib = np.empty((g, p, n, 4), np.uint8)
        nib[..., 0::2] = words & 0xF
        nib[..., 1::2] = words >> 4
        vals = E2M1[nib]
    vals = vals * np.repeat(np.exp2(scales.astype(np.float64) - 127.0), 8, axis=1)[..., None]
    return vals.transpose(0, 1, 3, 2).reshape(g * 512, n)

def pack4(w):
    words, scales = pack_weight(w, "e2m1")
    return words.reshape(words.shape[0], 128, -1), scales


def unpack4(words, scales):
    return unpack_weight(words.reshape(words.shape[0], 128, -1, 2), scales, "e2m1")


def kspread(k):
    return np.exp2(np.repeat(np.random.randint(-6, 7, k // 32), 32).astype(np.float64))


B, L, C, H, BLK = 2, 256, 4096, 16, 128
D = C // H
MAX_SCALE_MUL = np.log(100.0)
EPS = 1e-12


def l2norm(t):
    n = np.sqrt(np.sum(t * t, axis=-1, keepdims=True))
    return t / np.maximum(n, EPS)


def setup_inputs():
    s = kspread(C)
    lsm = np.linspace(np.log(4.0), MAX_SCALE_MUL + 1.0, H) + 0.05 * np.random.standard_normal(H)
    x = np.random.standard_normal((B, L, C)) * s
    x_words, x_scales = pack4(np.ascontiguousarray(x.reshape(B * L, C).T))
    w = np.random.standard_normal((3 * C, C)) / np.sqrt(C) / s[None, :]
    words, scales = pack4(np.ascontiguousarray(w.T))
    q_bias = bf(np.random.standard_normal(C) * 0.3)
    v_bias = bf(np.random.standard_normal(C) * 0.3)
    return {"x_words": x_words,
            "x_scales": x_scales,
            "W_qkv_words": words,
            "W_qkv_scales": scales,
            "q_bias": q_bias,
            "v_bias": v_bias,
            "log_scale_mul": bf(lsm.reshape(1, H, 1, 1))}


def reference(x_words, x_scales, W_qkv_words, W_qkv_scales, q_bias, v_bias, log_scale_mul):
    qb = f64(q_bias)
    bias = np.concatenate([qb, np.zeros_like(qb), f64(v_bias)])
    xv = unpack4(x_words, x_scales).T.reshape(B, L, C)
    qkv = (xv @ unpack4(W_qkv_words, W_qkv_scales)) + bias
    qkv = qkv.reshape(B, L, 3, H, D)
    q, k, v = np.moveaxis(qkv, 2, 0)
    q = np.swapaxes(q, 1, 2)
    k = np.swapaxes(k, 1, 2)
    v = np.swapaxes(v, 1, 2)
    scale_mul = np.exp(np.minimum(f64(log_scale_mul), MAX_SCALE_MUL))
    q = l2norm(q) * scale_mul
    k = l2norm(k)
    return q, k, v

@@ -1,0 +1,233 @@
+import math
+from contextlib import ExitStack
+
+import concourse.mybir as mybir
+
+F32 = mybir.dt.float32
+BF16 = mybir.dt.bfloat16
+I32 = mybir.dt.int32
+U8 = mybir.dt.uint8
+FP4X4 = mybir.dt.float4_e2m1fn_x4
+ALU = mybir.AluOpType
+ACT = mybir.ActivationFunctionType
+
+P = 128
+BATCH, SEQ, C, HEADS = 2, 256, 4096, 16
+D = C // HEADS
+TOK = BATCH * SEQ
+PASSES = C // 512
+NB = 512
+CHUNK = 1024
+BUFS = 6
+MT = TOK // P
+FLOPS = 2 * TOK * C * 3 * C
+WARM = 7
+
+
+def tile_selfattention_pa_kernel(
+    tc, x_words, x_scales, W_words, W_scales, q_bias, v_bias, log_scale_mul, out_q, out_k, out_v
+):
+    nc = tc.nc
+    with ExitStack() as ctx:
+        keep = ctx.enter_context(tc.tile_pool(name="keep", bufs=1))
+        outs = ctx.enter_context(tc.tile_pool(name="outs", bufs=12))
+        small = ctx.enter_context(tc.tile_pool(name="small", bufs=6))
+        psum = ctx.enter_context(tc.psum_pool(name="psum", bufs=8))
+
+        xc = keep.tile([P, PASSES, 2 * TOK], U8, name="xc", align_bytes=256)
+        xs = keep.tile([P, PASSES, TOK], U8, name="xs", align_bytes=256)
+        wc = []
+        ws = []
+        for i in range(BUFS):
+            wc_tile = keep.tile([P, PASSES, 2 * CHUNK], U8, name="wc%d" % i, align_bytes=256)
+            ws_tile = keep.tile([P, PASSES, CHUNK], U8, name="ws%d" % i, align_bytes=256)
+            wc.append(wc_tile)
+            ws.append(ws_tile)
+        bias_sb = keep.tile([P, 2 * C], BF16, name="bias_sb")
+        lsm = keep.tile([P, HEADS], BF16, name="lsm")
+        lsm_c = keep.tile([P, HEADS], F32, name="lsm_c")
+        smul = keep.tile([P, HEADS], F32, name="smul")
+        warm = keep.tile([P, NB], BF16, name="warm", align_bytes=64)
+
+        ctx.enter_context(tc.manual_schedule())
+
+        order = [4, 5, 6, 7, 0, 1, 2, 3, 8, 9, 10, 11]
+
+        def zero(tile, g0, g1):
+            nc.vector.memset(tile[:, g0:g1, :].bitcast(I32), 0)
+
+        def load_xc(g0, g1):
+            nc.sync.dma_start(
+                out=xc[:, g0:g1, :].bitcast(I32),
+                in_=x_words[g0:g1, :, :].bitcast(I32).rearrange("g p n -> p g n"),
+            )
+
+        def load_wc(j, g0, g1):
+            c0 = order[j] * CHUNK
+            nc.sync.dma_start(
+                out=wc[j % BUFS][:, g0:g1, :].bitcast(I32),
+                in_=W_words[g0:g1, :, 2 * c0 : 2 * (c0 + CHUNK)].bitcast(I32).rearrange("g p n -> p g n"),
+            )
+
+        def load_xs(q, g0, g1):
+            nc.sync.dma_start(
+                out=xs[32 * q : 32 * q + 4, g0:g1, :].bitcast(I32),
+                in_=x_scales[g0:g1, 4 * q : 4 * q + 4, :].bitcast(I32).rearrange("g r n -> r g n"),
+            )
+
+        def load_ws(j, q, g0, g1):
+            c0 = order[j] * CHUNK
+            nc.sync.dma_start(
+                out=ws[j % BUFS][32 * q : 32 * q + 4, g0:g1, :].bitcast(I32),
+                in_=W_scales[g0:g1, 4 * q : 4 * q + 4, c0 : c0 + CHUNK].bitcast(I32).rearrange("g r n -> r g n"),
+            )
+
+        def load_ws_r(j, r):
+            c0 = order[j] * CHUNK
+            nc.sync.dma_start(
+                out=ws[j % BUFS][r : P : 32, :, :].bitcast(I32),
+                in_=W_scales[:, r : 16 : 4, c0 : c0 + CHUNK].bitcast(I32).rearrange("g q n -> q g n"),
+            )
+
+        def load_chunk(j):
+            load_ws_r(j, 0)
+            load_wc(j, 0, 4)
+            load_ws_r(j, 1)
+            load_wc(j, 4, 8)
+            load_ws_r(j, 2)
+            load_ws_r(j, 3)
+
+        def passes(bank, j, m, n0, n, g0, g1):
+            for g in range(g0, g1):
+                nc.tensor.matmul_mx(
+                    out=bank[:, 0:n],
+                    lhsT=xc[:, g, 256 * m : 256 * (m + 1)].bitcast(FP4X4),
+                    lhsT_scale=xs[:, g, P * m : P * (m + 1)],
+                    rhs=wc[j % BUFS][:, g, 2 * n0 : 2 * (n0 + n)].bitcast(FP4X4),
+                    rhs_scale=ws[j % BUFS][:, g, n0 : n0 + n],
+                    start=(g == 0),
+                    stop=(g == PASSES - 1),
+                )
+
+        pending = []
+
+        def stage_a(bank, j, m, n0, n):
+            col = order[j] * CHUNK + n0
+            kind = col // C
+            col = col % C
+            heads = n // D
+            o = outs.tile([P, n], F32, name="o")
+            if kind != 1:
+                b0 = col if kind == 0 else C + col
+                nc.vector.tensor_tensor(out=o[:], in0=bank[:, 0:n], in1=bias_sb[:, b0 : b0 + n], op=ALU.add)
+            if kind == 2:
+                store(o, kind, m, col // D, heads, j)
+                return
+            ss = small.tile([P, heads], F32, name="ss")
+            for h in range(heads):
+                junk = small.tile([P, D], BF16, name="junk")
+                src = bank if kind == 1 else o
+                nc.scalar.activation(
+                    out=junk[:], in_=src[:, h * D : (h + 1) * D], func=ACT.Square, accum_out=ss[:, h : h + 1]
+                )
+            nrm = small.tile([P, heads], F32, name="nrm")
+            nc.scalar.activation(out=nrm[:], in_=ss[:], func=ACT.Sqrt)
+            pending.append((bank, o, nrm, kind, m, col // D, heads, j))
+
+        def stage_b():
+            bank, o, nrm, kind, m, h0, heads, j = pending.pop(0)
+            big = small.tile([P, heads], F32, name="big")
+            nc.vector.tensor_scalar_max(big[:], nrm[:], 1e-12)
+            inv = small.tile([P, heads], F32, name="inv")
+            nc.vector.reciprocal(out=inv[:], in_=big[:])
+            for h in range(heads):
+                cols = slice(h * D, (h + 1) * D)
+                if kind == 0:
+                    nc.vector.tensor_scalar(
+                        out=o[:, cols], in0=o[:, cols], scalar1=inv[:, h : h + 1],
+                        scalar2=smul[:, h0 + h : h0 + h + 1], op0=ALU.mult, op1=ALU.mult,
+                    )
+                else:
+                    nc.vector.tensor_scalar(
+                        out=o[:, cols], in0=bank[:, cols], scalar1=inv[:, h : h + 1], scalar2=None, op0=ALU.mult
+                    )
+            store(o, kind, m, h0, heads, j)
+
+        def store(o, kind, m, h0, heads, j):
+            dst = (out_q, out_k, out_v)[kind]
+            t0 = P * (m % 2)
+            engine = nc.sync if j == len(order) - 1 else nc.gpsimd
+            engine.dma_start(
+                out=dst[m // 2, h0 : h0 + heads, t0 : t0 + P, :].rearrange("h t d -> t h d"),
+                in_=o[:].rearrange("p (h d) -> p h d", h=heads),
+            )
+
+        def finish(bank, j, m, n0, n):
+            stage_a(bank, j, m, n0, n)
+            while len(pending) > 1 or (pending and order[j] >= 8):
+                stage_b()
+
+        def load_bias(i):
+            src = q_bias if i < 4 else v_bias
+            c0 = (i % 4) * CHUNK
+            nc.gpsimd.dma_start(
+                out=bias_sb[:, i * CHUNK : (i + 1) * CHUNK], in_=src[c0 : c0 + CHUNK].partition_broadcast(P)
+            )
+
+        nc.gpsimd.dma_start(out=lsm[:], in_=log_scale_mul.rearrange("a h b c -> (a h b c)").partition_broadcast(P))
+        load_xc(0, 1)
+        load_wc(0, 0, 1)
+        zero(xs, 0, 2)
+        zero(ws[0], 0, 2)
+        nc.vector.memset(warm[:], 0.0)
+        zero(xs, 2, 8)
+        zero(ws[0], 2, 8)
+        nc.vector.tensor_scalar_min(lsm_c[:], lsm[:], math.log(100.0))
+        nc.scalar.activation(out=smul[:], in_=lsm_c[:], func=ACT.Exp)
+        for i in range(1, BUFS):
+            zero(ws[i], 0, 8)
+        for q in range(4):
+            load_xs(q, 0, 2)
+        for q in range(4):
+            load_ws(0, q, 0, 2)
+        load_xc(1, 4)
+        load_wc(0, 1, 3)
+        for q in range(4):
+            load_xs(q, 2, 8)
+        for q in range(4):
+            load_ws(0, q, 2, 8)
+        load_wc(0, 3, 5)
+        load_xc(4, 8)
+        load_wc(0, 5, 8)
+        for j in range(1, BUFS):
+            load_chunk(j)
+
+        bank = psum.tile([P, NB], F32, name="bank")
+        for i in range(WARM):
+            nc.tensor.matmul(bank[:], warm[:, 0:P], warm[:], start=True, stop=True)
+
+        groups = [(n0, m) for n0 in range(0, CHUNK, NB) for m in range(MT)]
+        banks = []
+        for n0, m in groups:
+            bank = psum.tile([P, NB], F32, name="bank")
+            banks.append(bank)
+        for g in range(4):
+            for i, (n0, m) in enumerate(groups):
+                passes(banks[i], 0, m, n0, NB, g, g + 1)
+        for i, (n0, m) in enumerate(groups):
+            passes(banks[i], 0, m, n0, NB, 4, PASSES)
+            finish(banks[i], 0, m, n0, NB)
+
+        for j in range(1, len(order)):
+            if j + BUFS - 1 < len(order):
+                load_chunk(j + BUFS - 1)
+            if j <= 8:
+                load_bias(j - 1)
+            for n0, m in groups:
+                widths = [NB]
+                if j == len(order) - 1 and (n0, m) == groups[-1]:
+                    widths = [NB // 2, NB // 2]
+                for i, n in enumerate(widths):
+                    bank = psum.tile([P, NB], F32, name="bank")
+                    passes(bank, j, m, n0 + i * n, n, 0, PASSES)
+                    finish(bank, j, m, n0 + i * n, n)

@@ -82,20 +82,11 @@ def tile_selfattention_pa_kernel(
                 in_=W_scales[g0:g1, 4 * q : 4 * q + 4, c0 : c0 + CHUNK].bitcast(I32).rearrange("g r n -> r g n"),
             )
 
-        def load_ws_r(j, r):
-            c0 = order[j] * CHUNK
-            nc.sync.dma_start(
-                out=ws[j % BUFS][r : P : 32, :, :].bitcast(I32),
-                in_=W_scales[:, r : 16 : 4, c0 : c0 + CHUNK].bitcast(I32).rearrange("g q n -> q g n"),
-            )
-
         def load_chunk(j):
-            load_ws_r(j, 0)
+            for q in (0, 2, 1, 3):
+                load_ws(j, q, 0, PASSES)
             load_wc(j, 0, 4)
-            load_ws_r(j, 1)
-            load_wc(j, 4, 8)
-            load_ws_r(j, 2)
-            load_ws_r(j, 3)
+            load_wc(j, 4, PASSES)
 
         def passes(bank, j, m, n0, n, g0, g1):
             for g in range(g0, g1):
@@ -174,7 +165,6 @@ def tile_selfattention_pa_kernel(
                 out=bias_sb[:, i * CHUNK : (i + 1) * CHUNK], in_=src[c0 : c0 + CHUNK].partition_broadcast(P)
             )
 
-        nc.gpsimd.dma_start(out=lsm[:], in_=log_scale_mul.rearrange("a h b c -> (a h b c)").partition_broadcast(P))
         load_xc(0, 1)
         load_wc(0, 0, 1)
         zero(xs, 0, 2)
@@ -182,8 +172,6 @@ def tile_selfattention_pa_kernel(
         nc.vector.memset(warm[:], 0.0)
         zero(xs, 2, 8)
         zero(ws[0], 2, 8)
-        nc.vector.tensor_scalar_min(lsm_c[:], lsm[:], math.log(100.0))
-        nc.scalar.activation(out=smul[:], in_=lsm_c[:], func=ACT.Exp)
         for i in range(1, BUFS):
             zero(ws[i], 0, 8)
         for q in range(4):
@@ -218,11 +206,16 @@ def tile_selfattention_pa_kernel(
             passes(banks[i], 0, m, n0, NB, 4, PASSES)
             finish(banks[i], 0, m, n0, NB)
 
+        nc.gpsimd.dma_start(out=lsm[:], in_=log_scale_mul.rearrange("a h b c -> (a h b c)").partition_broadcast(P))
+
         for j in range(1, len(order)):
             if j + BUFS - 1 < len(order):
                 load_chunk(j + BUFS - 1)
             if j <= 8:
                 load_bias(j - 1)
+            if j == 2:
+                nc.vector.tensor_scalar_min(lsm_c[:], lsm[:], math.log(100.0))
+                nc.scalar.activation(out=smul[:], in_=lsm_c[:], func=ACT.Exp)
             for n0, m in groups:
                 widths = [NB]
                 if j == len(order) - 1 and (n0, m) == groups[-1]:

@@ -108,7 +108,9 @@ def tile_selfattention_pa_kernel(
             col = col % C
             heads = n // D
             o = outs.tile([P, n], F32, name="o")
-            if kind != 1:
+            if kind == 1:
+                nc.vector.tensor_copy(out=o[:], in_=bank[:, 0:n])
+            else:
                 b0 = col if kind == 0 else C + col
                 nc.vector.tensor_tensor(out=o[:], in0=bank[:, 0:n], in1=bias_sb[:, b0 : b0 + n], op=ALU.add)
             if kind == 2:
@@ -117,16 +119,15 @@ def tile_selfattention_pa_kernel(
             ss = small.tile([P, heads], F32, name="ss")
             for h in range(heads):
                 junk = small.tile([P, D], BF16, name="junk")
-                src = bank if kind == 1 else o
                 nc.scalar.activation(
-                    out=junk[:], in_=src[:, h * D : (h + 1) * D], func=ACT.Square, accum_out=ss[:, h : h + 1]
+                    out=junk[:], in_=o[:, h * D : (h + 1) * D], func=ACT.Square, accum_out=ss[:, h : h + 1]
                 )
             nrm = small.tile([P, heads], F32, name="nrm")
             nc.scalar.activation(out=nrm[:], in_=ss[:], func=ACT.Sqrt)
-            pending.append((bank, o, nrm, kind, m, col // D, heads, j))
+            pending.append((o, nrm, kind, m, col // D, heads, j))
 
         def stage_b():
-            bank, o, nrm, kind, m, h0, heads, j = pending.pop(0)
+            o, nrm, kind, m, h0, heads, j = pending.pop(0)
             big = small.tile([P, heads], F32, name="big")
             nc.vector.tensor_scalar_max(big[:], nrm[:], 1e-12)
             inv = small.tile([P, heads], F32, name="inv")
@@ -140,7 +141,7 @@ def tile_selfattention_pa_kernel(
                     )
                 else:
                     nc.vector.tensor_scalar(
-                        out=o[:, cols], in0=bank[:, cols], scalar1=inv[:, h : h + 1], scalar2=None, op0=ALU.mult
+                        out=o[:, cols], in0=o[:, cols], scalar1=inv[:, h : h + 1], scalar2=None, op0=ALU.mult
                     )
             store(o, kind, m, h0, heads, j)
 
@@ -167,26 +168,24 @@ def tile_selfattention_pa_kernel(
 
         load_xc(0, 1)
         load_wc(0, 0, 1)
-        zero(xs, 0, 2)
-        zero(ws[0], 0, 2)
-        nc.vector.memset(warm[:], 0.0)
-        zero(xs, 2, 8)
-        zero(ws[0], 2, 8)
+        for g0 in range(0, PASSES, 2):
+            zero(xs, g0, g0 + 2)
+            zero(ws[0], g0, g0 + 2)
+            if g0 == 0:
+                nc.vector.memset(warm[:], 0.0)
         for i in range(1, BUFS):
-            zero(ws[i], 0, 8)
-        for q in range(4):
-            load_xs(q, 0, 2)
-        for q in range(4):
-            load_ws(0, q, 0, 2)
-        load_xc(1, 4)
-        load_wc(0, 1, 3)
-        for q in range(4):
-            load_xs(q, 2, 8)
-        for q in range(4):
-            load_ws(0, q, 2, 8)
-        load_wc(0, 3, 5)
-        load_xc(4, 8)
-        load_wc(0, 5, 8)
+            zero(ws[i], 0, PASSES)
+        for g0 in range(0, PASSES, 2):
+            if g0 > 0:
+                load_xc(g0, g0 + 2)
+                load_wc(0, g0, g0 + 2)
+            for q in range(4):
+                load_xs(q, g0, g0 + 2)
+            for q in range(4):
+                load_ws(0, q, g0, g0 + 2)
+            if g0 == 0:
+                load_xc(1, 2)
+                load_wc(0, 1, 2)
         for j in range(1, BUFS):
             load_chunk(j)
 
@@ -199,11 +198,11 @@ def tile_selfattention_pa_kernel(
         for n0, m in groups:
             bank = psum.tile([P, NB], F32, name="bank")
             banks.append(bank)
-        for g in range(4):
+        for g in range(6):
             for i, (n0, m) in enumerate(groups):
                 passes(banks[i], 0, m, n0, NB, g, g + 1)
         for i, (n0, m) in enumerate(groups):
-            passes(banks[i], 0, m, n0, NB, 4, PASSES)
+            passes(banks[i], 0, m, n0, NB, 6, PASSES)
             finish(banks[i], 0, m, n0, NB)
 
         nc.gpsimd.dma_start(out=lsm[:], in_=log_scale_mul.rearrange("a h b c -> (a h b c)").partition_broadcast(P))

@@ -34,15 +34,17 @@ def tile_selfattention_pa_kernel(
         small = ctx.enter_context(tc.tile_pool(name="small", bufs=6))
         psum = ctx.enter_context(tc.psum_pool(name="psum", bufs=8))
 
-        xc = keep.tile([P, PASSES, 2 * TOK], U8, name="xc", align_bytes=256)
-        xs = keep.tile([P, PASSES, TOK], U8, name="xs", align_bytes=256)
+        def operand(name, width, shift):
+            flat = keep.tile([P, PASSES * width + 256], U8, name=name, align_bytes=256)
+            return flat[:, shift : shift + PASSES * width].rearrange("p (g n) -> p g n", g=PASSES)
+
+        xc = operand("xc", 2 * TOK, 128)
+        xs = operand("xs", TOK, 192)
         wc = []
         ws = []
         for i in range(BUFS):
-            wc_tile = keep.tile([P, PASSES, 2 * CHUNK], U8, name="wc%d" % i, align_bytes=256)
-            ws_tile = keep.tile([P, PASSES, CHUNK], U8, name="ws%d" % i, align_bytes=256)
-            wc.append(wc_tile)
-            ws.append(ws_tile)
+            wc.append(operand("wc%d" % i, 2 * CHUNK, 0))
+            ws.append(operand("ws%d" % i, CHUNK, 64))
         bias_sb = keep.tile([P, 2 * C], BF16, name="bias_sb")
         lsm = keep.tile([P, HEADS], BF16, name="lsm")
         lsm_c = keep.tile([P, HEADS], F32, name="lsm_c")
@@ -62,11 +64,11 @@ def tile_selfattention_pa_kernel(
                 in_=x_words[g0:g1, :, :].bitcast(I32).rearrange("g p n -> p g n"),
             )
 
-        def load_wc(j, g0, g1):
+        def load_wc(j, g0, g1, n0=0, n1=CHUNK):
             c0 = order[j] * CHUNK
             nc.sync.dma_start(
-                out=wc[j % BUFS][:, g0:g1, :].bitcast(I32),
-                in_=W_words[g0:g1, :, 2 * c0 : 2 * (c0 + CHUNK)].bitcast(I32).rearrange("g p n -> p g n"),
+                out=wc[j % BUFS][:, g0:g1, 2 * n0 : 2 * n1].bitcast(I32),
+                in_=W_words[g0:g1, :, 2 * (c0 + n0) : 2 * (c0 + n1)].bitcast(I32).rearrange("g p n -> p g n"),
             )
 
         def load_xs(q, g0, g1):
@@ -167,7 +169,7 @@ def tile_selfattention_pa_kernel(
             )
 
         load_xc(0, 1)
-        load_wc(0, 0, 1)
+        load_wc(0, 0, 1, 0, NB)
         for g0 in range(0, PASSES, 2):
             zero(xs, g0, g0 + 2)
             zero(ws[0], g0, g0 + 2)
@@ -184,6 +186,7 @@ def tile_selfattention_pa_kernel(
             for q in range(4):
                 load_ws(0, q, g0, g0 + 2)
             if g0 == 0:
+                load_wc(0, 0, 1, NB, CHUNK)
                 load_xc(1, 2)
                 load_wc(0, 1, 2)
         for j in range(1, BUFS):

import math
from contextlib import ExitStack

import concourse.mybir as mybir

F32 = mybir.dt.float32
BF16 = mybir.dt.bfloat16
I32 = mybir.dt.int32
U8 = mybir.dt.uint8
FP4X4 = mybir.dt.float4_e2m1fn_x4
ALU = mybir.AluOpType
ACT = mybir.ActivationFunctionType

P = 128
BATCH, SEQ, C, HEADS = 2, 256, 4096, 16
D = C // HEADS
TOK = BATCH * SEQ
PASSES = C // 512
NB = 512
CHUNK = 1024
BUFS = 6
MT = TOK // P
FLOPS = 2 * TOK * C * 3 * C
WARM = 7


def tile_selfattention_pa_kernel(
    tc, x_words, x_scales, W_words, W_scales, q_bias, v_bias, log_scale_mul, out_q, out_k, out_v
):
    nc = tc.nc
    with ExitStack() as ctx:
        keep = ctx.enter_context(tc.tile_pool(name="keep", bufs=1))
        outs = ctx.enter_context(tc.tile_pool(name="outs", bufs=12))
        small = ctx.enter_context(tc.tile_pool(name="small", bufs=6))
        psum = ctx.enter_context(tc.psum_pool(name="psum", bufs=8))

        def operand(name, width, shift):
            flat = keep.tile([P, PASSES * width + 256], U8, name=name, align_bytes=256)
            return flat[:, shift : shift + PASSES * width].rearrange("p (g n) -> p g n", g=PASSES)

        xc = operand("xc", 2 * TOK, 128)
        xs = operand("xs", TOK, 192)
        wc = []
        ws = []
        for i in range(BUFS):
            wc.append(operand("wc%d" % i, 2 * CHUNK, 0))
            ws.append(operand("ws%d" % i, CHUNK, 64))
        bias_sb = keep.tile([P, 2 * C], BF16, name="bias_sb")
        lsm = keep.tile([P, HEADS], BF16, name="lsm")
        lsm_c = keep.tile([P, HEADS], F32, name="lsm_c")
        smul = keep.tile([P, HEADS], F32, name="smul")
        warm = keep.tile([P, NB], BF16, name="warm", align_bytes=64)

        ctx.enter_context(tc.manual_schedule())

        order = [4, 5, 6, 7, 0, 1, 2, 3, 8, 9, 10, 11]

        def zero(tile, g0, g1):
            nc.vector.memset(tile[:, g0:g1, :].bitcast(I32), 0)

        def load_xc(g0, g1):
            nc.sync.dma_start(
                out=xc[:, g0:g1, :].bitcast(I32),
                in_=x_words[g0:g1, :, :].bitcast(I32).rearrange("g p n -> p g n"),
            )

        def load_wc(j, g0, g1, n0=0, n1=CHUNK):
            c0 = order[j] * CHUNK
            nc.sync.dma_start(
                out=wc[j % BUFS][:, g0:g1, 2 * n0 : 2 * n1].bitcast(I32),
                in_=W_words[g0:g1, :, 2 * (c0 + n0) : 2 * (c0 + n1)].bitcast(I32).rearrange("g p n -> p g n"),
            )

        def load_xs(q, g0, g1):
            nc.sync.dma_start(
                out=xs[32 * q : 32 * q + 4, g0:g1, :].bitcast(I32),
                in_=x_scales[g0:g1, 4 * q : 4 * q + 4, :].bitcast(I32).rearrange("g r n -> r g n"),
            )

        def load_ws(j, q, g0, g1):
            c0 = order[j] * CHUNK
            nc.sync.dma_start(
                out=ws[j % BUFS][32 * q : 32 * q + 4, g0:g1, :].bitcast(I32),
                in_=W_scales[g0:g1, 4 * q : 4 * q + 4, c0 : c0 + CHUNK].bitcast(I32).rearrange("g r n -> r g n"),
            )

        def load_chunk(j):
            for q in (0, 2, 1, 3):
                load_ws(j, q, 0, PASSES)
            load_wc(j, 0, 4)
            load_wc(j, 4, PASSES)

        def passes(bank, j, m, n0, n, g0, g1):
            for g in range(g0, g1):
                nc.tensor.matmul_mx(
                    out=bank[:, 0:n],
                    lhsT=xc[:, g, 256 * m : 256 * (m + 1)].bitcast(FP4X4),
                    lhsT_scale=xs[:, g, P * m : P * (m + 1)],
                    rhs=wc[j % BUFS][:, g, 2 * n0 : 2 * (n0 + n)].bitcast(FP4X4),
                    rhs_scale=ws[j % BUFS][:, g, n0 : n0 + n],
                    start=(g == 0),
                    stop=(g == PASSES - 1),
                )

        pending = []

        def stage_a(bank, j, m, n0, n):
            col = order[j] * CHUNK + n0
            kind = col // C
            col = col % C
            heads = n // D
            o = outs.tile([P, n], F32, name="o")
            if kind == 1:
                nc.vector.tensor_copy(out=o[:], in_=bank[:, 0:n])
            else:
                b0 = col if kind == 0 else C + col
                nc.vector.tensor_tensor(out=o[:], in0=bank[:, 0:n], in1=bias_sb[:, b0 : b0 + n], op=ALU.add)
            if kind == 2:
                store(o, kind, m, col // D, heads, j)
                return
            ss = small.tile([P, heads], F32, name="ss")
            for h in range(heads):
                junk = small.tile([P, D], BF16, name="junk")
                nc.scalar.activation(
                    out=junk[:], in_=o[:, h * D : (h + 1) * D], func=ACT.Square, accum_out=ss[:, h : h + 1]
                )
            nrm = small.tile([P, heads], F32, name="nrm")
            nc.scalar.activation(out=nrm[:], in_=ss[:], func=ACT.Sqrt)
            pending.append((o, nrm, kind, m, col // D, heads, j))

        def stage_b():
            o, nrm, kind, m, h0, heads, j = pending.pop(0)
            big = small.tile([P, heads], F32, name="big")
            nc.vector.tensor_scalar_max(big[:], nrm[:], 1e-12)
            inv = small.tile([P, heads], F32, name="inv")
            nc.vector.reciprocal(out=inv[:], in_=big[:])
            for h in range(heads):
                cols = slice(h * D, (h + 1) * D)
                if kind == 0:
                    nc.vector.tensor_scalar(
                        out=o[:, cols], in0=o[:, cols], scalar1=inv[:, h : h + 1],
                        scalar2=smul[:, h0 + h : h0 + h + 1], op0=ALU.mult, op1=ALU.mult,
                    )
                else:
                    nc.vector.tensor_scalar(
                        out=o[:, cols], in0=o[:, cols], scalar1=inv[:, h : h + 1], scalar2=None, op0=ALU.mult
                    )
            store(o, kind, m, h0, heads, j)

        def store(o, kind, m, h0, heads, j):
            dst = (out_q, out_k, out_v)[kind]
            t0 = P * (m % 2)
            engine = nc.sync if j == len(order) - 1 else nc.gpsimd
            engine.dma_start(
                out=dst[m // 2, h0 : h0 + heads, t0 : t0 + P, :].rearrange("h t d -> t h d"),
                in_=o[:].rearrange("p (h d) -> p h d", h=heads),
            )

        def finish(bank, j, m, n0, n):
            stage_a(bank, j, m, n0, n)
            while len(pending) > 1 or (pending and order[j] >= 8):
                stage_b()

        def load_bias(i):
            src = q_bias if i < 4 else v_bias
            c0 = (i % 4) * CHUNK
            nc.gpsimd.dma_start(
                out=bias_sb[:, i * CHUNK : (i + 1) * CHUNK], in_=src[c0 : c0 + CHUNK].partition_broadcast(P)
            )

        load_xc(0, 1)
        load_wc(0, 0, 1, 0, NB)
        for g0 in range(0, PASSES, 2):
            zero(xs, g0, g0 + 2)
            zero(ws[0], g0, g0 + 2)
            if g0 == 0:
                nc.vector.memset(warm[:], 0.0)
        for i in range(1, BUFS):
            zero(ws[i], 0, PASSES)
        for g0 in range(0, PASSES, 2):
            if g0 > 0:
                load_xc(g0, g0 + 2)
                load_wc(0, g0, g0 + 2)
            for q in range(4):
                load_xs(q, g0, g0 + 2)
            for q in range(4):
                load_ws(0, q, g0, g0 + 2)
            if g0 == 0:
                load_wc(0, 0, 1, NB, CHUNK)
                load_xc(1, 2)
                load_wc(0, 1, 2)
        for j in range(1, BUFS):
            load_chunk(j)

        bank = psum.tile([P, NB], F32, name="bank")
        for i in range(WARM):
            nc.tensor.matmul(bank[:], warm[:, 0:P], warm[:], start=True, stop=True)

        groups = [(n0, m) for n0 in range(0, CHUNK, NB) for m in range(MT)]
        banks = []
        for n0, m in groups:
            bank = psum.tile([P, NB], F32, name="bank")
            banks.append(bank)
        for g in range(6):
            for i, (n0, m) in enumerate(groups):
                passes(banks[i], 0, m, n0, NB, g, g + 1)
        for i, (n0, m) in enumerate(groups):
            passes(banks[i], 0, m, n0, NB, 6, PASSES)
            finish(banks[i], 0, m, n0, NB)

        nc.gpsimd.dma_start(out=lsm[:], in_=log_scale_mul.rearrange("a h b c -> (a h b c)").partition_broadcast(P))

        for j in range(1, len(order)):
            if j + BUFS - 1 < len(order):
                load_chunk(j + BUFS - 1)
            if j <= 8:
                load_bias(j - 1)
            if j == 2:
                nc.vector.tensor_scalar_min(lsm_c[:], lsm[:], math.log(100.0))
                nc.scalar.activation(out=smul[:], in_=lsm_c[:], func=ACT.Exp)
            for n0, m in groups:
                widths = [NB]
                if j == len(order) - 1 and (n0, m) == groups[-1]:
                    widths = [NB // 2, NB // 2]
                for i, n in enumerate(widths):
                    bank = psum.tile([P, NB], F32, name="bank")
                    passes(bank, j, m, n0 + i * n, n, 0, PASSES)
                    finish(bank, j, m, n0 + i * n, n)
